import numpy as np
import ml_dtypes


def mxq(x, axis, fmt="e4m3"):
    dtype, down = {"e4m3": (ml_dtypes.float8_e4m3fn, 7), "e5m2": (ml_dtypes.float8_e5m2, 14)}[fmt]
    v = np.moveaxis(np.asarray(x, np.float32).astype(ml_dtypes.bfloat16).astype(np.float64), axis, -1)
    blocks = v.reshape(v.shape[:-1] + (-1, 32))
    amax = np.abs(blocks).max(-1, keepdims=True)
    byte = np.maximum(np.where(amax > 0, np.frexp(amax)[1] - 1 + 127, 0) - down, 1)
    scale = np.exp2(byte - 127.0)
    codes = (blocks / scale).astype(np.float32).astype(dtype).astype(np.float64)
    return np.moveaxis((codes * scale).reshape(v.shape), -1, axis)


WIDE = False


def mx_kscale(k):
    if not WIDE:
        return np.ones(k)
    levels = np.array([10, -10, 5, -5, 0])
    a = np.random.permutation(np.resize(levels, k // 512 * 4)).reshape(k // 512, 4)
    idx = np.arange(k)
    return np.exp2(a[idx // 512, idx % 128 // 32])


BF16 = ml_dtypes.bfloat16


def bf(x):
    return np.asarray(x, np.float32).astype(BF16)


def f64(x):
    return np.asarray(x).astype(np.float64)


N, D, HOP = 1024, 512, 2
NW = HOP + 1


def setup_inputs():
    s = mx_kscale(N)
    u = s / s.min()
    g = u[None, :] / u[:, None]
    return {"A_p": bf(np.random.standard_normal((N, N)) / np.sqrt(N) * g),
            "x_p": bf(np.random.standard_normal((N, D)) / u[:, None]),
            "w_p": bf(1.0 + 0.1 * np.random.standard_normal((NW, 1)))}


def reference(A_p, x_p, w_p):
    ap = mxq(f64(A_p), 1, "e4m3")
    x = f64(x_p)
    wa, wb, wc = f64(w_p)
    feat_p = wa * x
    h1 = ap @ mxq(x, 0, "e4m3")
    feat_p = feat_p + wb * h1
    feat_p = feat_p + wc * (ap @ mxq(h1, 0, "e4m3"))
    return feat_p

@@ -1,0 +1,277 @@
+from contextlib import ExitStack
+
+import concourse.mybir as mybir
+from concourse.masks import make_identity
+
+F32 = mybir.dt.float32
+BF16 = mybir.dt.bfloat16
+U32 = mybir.dt.uint32
+U8 = mybir.dt.uint8
+FP8X4 = mybir.dt.float8_e4m3fn_x4
+ALU = mybir.AluOpType
+ACT = mybir.ActivationFunctionType
+
+P = 128
+N = 1024
+D = 512
+FLOPS = 2 * 2 * N * N * D
+
+PIN = True
+XS = 256
+GSPLIT = 1
+ATC_ENG = "SSSSSSSS"
+H1C_ENG = {(1, 0): "S", (1, 1): "S", (1, 2): "S", (1, 3): "S", (0, 0): "S", (0, 1): "S", (0, 2): "S", (0, 3): "S"}
+W0X_ENG = {(1, 0): "V", (1, 1): "V", (0, 0): "V", (0, 1): "V"}
+ACC_PATH = {(1, 0): "V", (1, 1): "V", (1, 2): "V", (1, 3): "V", (0, 0): "V", (0, 1): "V", (0, 2): "V", (0, 3): "V"}
+FIN_PATH = {(1, 0): "V", (1, 1): "V", (1, 2): "V", (1, 3): "V", (0, 0): "V", (0, 1): "V", (0, 2): "V", (0, 3): "V"}
+T_BANK = [4, 5, 6, 7, 4, 5, 6, 7]
+H_BANK = {(1, 0): 4, (1, 1): 5, (1, 2): 6, (1, 3): 7, (0, 0): 0, (0, 1): 1, (0, 2): 2, (0, 3): 3}
+O_BANK = {(1, 0): 4, (1, 1): 5, (1, 2): 6, (1, 3): 7, (0, 0): 0, (0, 1): 1, (0, 2): 2, (0, 3): 3}
+LOADS = ["x0", "x1", "A0", "A1", "A2", "A3"]
+ORDER = [
+    "xrgV0", "xrgS0", "xrgV1", "xrgS1", "xq0", "T0", "xq1", "T1", "ATc0", "w0x00", "ATc1", "T2",
+    "T3", "ATc2", "Aq0", "ATc3", "w0x01", "T4", "T5", "ATc4", "Aq1", "M0b0", "M0b1", "M0b2",
+    "ATc5", "w0x10", "M0b3", "T6", "Aq2", "T7", "ATc6", "M1b0", "w0x11", "M1b1", "ATc7", "M1b2",
+    "M1b3", "M2b0", "M2b1", "Aq3", "M2b2", "M2b3", "M3b0", "M3b1", "h1c00", "M3b2", "M3b3", "M4b0",
+    "M4b1", "acc00", "h1c01", "M5b0", "M5b1", "M6b0", "M6b1", "h1c02", "acc01", "M7b0", "M7b1", "M4b2",
+    "h1c03", "M4b3", "hq00", "M5b2", "M5b3", "acc02", "M6b2", "h1c10", "M6b3", "M7b2", "M7b3", "acc03",
+    "h1c11", "hq01", "h1c12", "hq10", "acc10", "h1c13", "O00", "acc11", "O01", "hq11", "O02", "fin00",
+    "O03", "acc12", "st00", "O10", "fin01", "O11", "acc13", "st01", "O12", "fin02", "O13", "fin03",
+    "st02", "fin10", "st03", "fin11", "st10", "fin12", "st11", "fin13", "st12", "st13",
+]
+
+
+def tile_simpa_pb_kernel(tc, A_p, x_p, w_p, out):
+    nc = tc.nc
+    with ExitStack() as ctx:
+        keep = ctx.enter_context(tc.tile_pool(name="keep", bufs=1))
+        psum = ctx.enter_context(tc.psum_pool(name="psum", bufs=1))
+        if PIN:
+            ctx.enter_context(tc.manual_schedule())
+
+        def copy_on(eng, dst, src):
+            if eng == "S":
+                nc.scalar.copy(out=dst, in_=src)
+            else:
+                nc.vector.tensor_copy(out=dst, in_=src)
+
+        w_bf = keep.tile([P, 3], BF16, name="w_bf")
+        nc.scalar.dma_start(out=w_bf[:], in_=w_p.rearrange("a b -> (a b)").partition_broadcast(P))
+        x_sb = {}
+        a_sb = {}
+        for name in LOADS:
+            i = int(name[1])
+            if name[0] == "x":
+                xt = keep.tile([P, 4, D], BF16, name="x_sb%d" % i)
+                nc.sync.dma_start(
+                    out=xt[:].rearrange("p (u e) d -> p u (e d)", e=2),
+                    in_=x_p[512 * i : 512 * (i + 1), :].rearrange("(u p e) d -> p u (e d)", u=2, e=2),
+                )
+                x_sb[i] = xt
+            else:
+                at = keep.tile([P, 2, N], BF16, name="a_sb%d" % i)
+                nc.sync.dma_start(
+                    out=at[:].rearrange("p e j -> p (e j)"),
+                    in_=A_p[256 * i : 256 * (i + 1), :].rearrange("(p e) j -> p (e j)", e=2),
+                )
+                a_sb[i] = at
+        ident = keep.tile([P, P], F32, name="ident")
+        make_identity(nc, ident[:])
+        w_f = keep.tile([P, 3], F32, name="w_f")
+        nc.vector.tensor_copy(out=w_f[:], in_=w_bf[:])
+
+        xg = {}
+        x_codes = {}
+        x_scales = {}
+
+        def do_xrg(eng, g):
+            if g not in xg:
+                xg[g] = keep.tile([P, D, 4], BF16, name="xg%d" % g, align_bytes=64)
+            lo, hi = (0, D - XS) if eng == "V" else (D - XS, D)
+            copy_on(
+                eng,
+                xg[g][:, lo:hi, :].rearrange("p (c i) t -> p c t i", i=4),
+                x_sb[g][:, :, lo:hi].rearrange("p t (c i) -> p c t i", i=4),
+            )
+
+        def do_xq(g):
+            x_codes[g] = keep.tile([P, D], U32, name="x_codes%d" % g, align_bytes=64)
+            x_scales[g] = keep.tile([P, D], U8, name="x_scales%d" % g, align_bytes=64)
+            nc.vector.quantize_mx(
+                out=x_codes[g][:].bitcast(FP8X4), scales=x_scales[g][:], in_=xg[g][:].rearrange("p d t -> p (d t)")
+            )
+
+        w0x = {}
+
+        def do_w0x(g, h):
+            t = keep.tile([P, 4, 256], F32, name="w0x%d%d" % (g, h))
+            src = x_sb[g][:, :, 256 * h : 256 * (h + 1)]
+            if W0X_ENG[(g, h)] == "S":
+                nc.scalar.activation(out=t[:], in_=src, func=ACT.Copy, scale=w_f[:, 0:1])
+            elif W0X_ENG[(g, h)] == "V":
+                nc.vector.tensor_scalar(out=t[:], in0=src, scalar1=w_f[:, 0:1], scalar2=None, op0=ALU.mult)
+            else:
+                nc.gpsimd.tensor_scalar(out=t[:], in0=src, scalar1=w_f[:, 0:1], scalar2=0.0, op0=ALU.mult, op1=ALU.add)
+            w0x[(g, h)] = t
+
+        tp = {}
+        ag = {}
+        a_codes = {}
+        a_scales = {}
+
+        def do_T(m):
+            c, e = divmod(m, 2)
+            t = psum.tile([P, 4, P], F32, tag="bank%d" % T_BANK[m], name="tp%d" % m)
+            aw = a_sb[c][:, e, :].bitcast(F32)
+            for k in range(4):
+                nc.tensor.transpose(t[:, k, :], aw[:, P * k : P * (k + 1)], ident[:])
+            tp[m] = t
+
+        def do_ATc(m):
+            c, e = divmod(m, 2)
+            if c not in ag:
+                ag[c] = keep.tile([P, 2, N], BF16, name="ag%d" % c, align_bytes=64)
+            copy_on(
+                ATC_ENG[m],
+                ag[c][:, e, :].bitcast(F32).rearrange("p (g i u) -> p g i u", g=2, u=2),
+                tp[m][:].rearrange("p (g u) i -> p g i u", u=2),
+            )
+
+        def do_Aq(c):
+            a_codes[c] = keep.tile([P, 512], U32, name="a_codes%d" % c, align_bytes=64)
+            a_scales[c] = keep.tile([P, 512], U8, name="a_scales%d" % c, align_bytes=64)
+            nc.vector.quantize_mx(
+                out=a_codes[c][:].bitcast(FP8X4), scales=a_scales[c][:], in_=ag[c][:].rearrange("p e k -> p (e k)")
+            )
+
+        def lhs(m, gp):
+            c, e = divmod(m, 2)
+            lo = (2 * e + gp) * P
+            return a_codes[c][:, lo : lo + P].bitcast(FP8X4), a_scales[c][:, lo : lo + P]
+
+        hb = {}
+
+        def do_M(m, b):
+            g, t = divmod(m, 4)
+            if (g, b) not in hb:
+                hb[(g, b)] = psum.tile([P, 4, P], F32, tag="bank%d" % H_BANK[(g, b)], name="hb%d%d" % (g, b))
+            for gp in range(2):
+                lt, ls = lhs(m, gp)
+                nc.tensor.matmul_mx(
+                    out=hb[(g, b)][:, t, :],
+                    lhsT=lt,
+                    lhsT_scale=ls,
+                    rhs=x_codes[gp][:, P * b : P * (b + 1)].bitcast(FP8X4),
+                    rhs_scale=x_scales[gp][:, P * b : P * (b + 1)],
+                    start=(gp == 0),
+                    stop=(gp == 1),
+                )
+
+        hg = {}
+        acc = {}
+        h1w = {}
+        h_codes = {}
+        h_scales = {}
+
+        def do_h1c(g, b):
+            h, r = divmod(b, 2)
+            if (g, h) not in hg:
+                hg[(g, h)] = keep.tile([P, 256, 4], BF16, name="hg%d%d" % (g, h), align_bytes=64)
+            copy_on(H1C_ENG[(g, b)], hg[(g, h)][:, P * r : P * (r + 1), :], hb[(g, b)][:].rearrange("p t d -> p d t"))
+
+        def do_h1w(g, b):
+            h1w[(g, b)] = keep.tile([P, 4, P], F32, name="h1w%d%d" % (g, b))
+            nc.scalar.activation(out=h1w[(g, b)][:], in_=hb[(g, b)][:], func=ACT.Copy, scale=w_f[:, 1:2])
+
+        def do_acc(g, b):
+            h, r = divmod(b, 2)
+            if (g, h) not in acc:
+                acc[(g, h)] = keep.tile([P, 4, 256], F32, name="acc%d%d" % (g, h))
+            dst = acc[(g, h)][:, :, P * r : P * (r + 1)]
+            prev = w0x[(g, h)][:, :, P * r : P * (r + 1)]
+            if ACC_PATH[(g, b)] == "V":
+                nc.vector.scalar_tensor_tensor(
+                    out=dst, in0=hb[(g, b)][:], scalar=w_f[:, 1:2], in1=prev, op0=ALU.mult, op1=ALU.add
+                )
+            else:
+                step = 4 // GSPLIT
+                for s in range(0, 4, step):
+                    nc.gpsimd.tensor_tensor(
+                        out=dst[:, s : s + step, :], in0=h1w[(g, b)][:, s : s + step, :], in1=prev[:, s : s + step, :], op=ALU.add
+                    )
+
+        def do_hq(g, h):
+            h_codes[(g, h)] = keep.tile([P, 256], U32, name="h_codes%d%d" % (g, h), align_bytes=64)
+            h_scales[(g, h)] = keep.tile([P, 256], U8, name="h_scales%d%d" % (g, h), align_bytes=64)
+            nc.vector.quantize_mx(
+                out=h_codes[(g, h)][:].bitcast(FP8X4),
+                scales=h_scales[(g, h)][:],
+                in_=hg[(g, h)][:].rearrange("p d t -> p (d t)"),
+            )
+
+        ob = {}
+        h2w = {}
+        o_sb = {}
+
+        def do_O(h, c):
+            ob[(h, c)] = psum.tile([P, 2, 256], F32, tag="bank%d" % O_BANK[(h, c)], name="ob%d%d" % (h, c))
+            for e in range(2):
+                for gp in range(2):
+                    lt, ls = lhs(2 * c + e, gp)
+                    nc.tensor.matmul_mx(
+                        out=ob[(h, c)][:, e, :],
+                        lhsT=lt,
+                        lhsT_scale=ls,
+                        rhs=h_codes[(gp, h)][:].bitcast(FP8X4),
+                        rhs_scale=h_scales[(gp, h)][:],
+                        start=(gp == 0),
+                        stop=(gp == 1),
+                    )
+
+        def do_h2w(h, c):
+            h2w[(h, c)] = keep.tile([P, 2, 256], F32, name="h2w%d%d" % (h, c))
+            nc.scalar.activation(out=h2w[(h, c)][:], in_=ob[(h, c)][:], func=ACT.Copy, scale=w_f[:, 2:3])
+
+        def do_fin(h, c):
+            g, u = divmod(c, 2)
+            o_sb[(h, c)] = keep.tile([P, 2, 256], F32, name="o%d%d" % (h, c))
+            prev = acc[(g, h)][:, 2 * u : 2 * u + 2, :]
+            if FIN_PATH[(h, c)] == "V":
+                nc.vector.scalar_tensor_tensor(
+                    out=o_sb[(h, c)][:], in0=ob[(h, c)][:], scalar=w_f[:, 2:3], in1=prev, op0=ALU.mult, op1=ALU.add
+                )
+            else:
+                step = 2 // min(GSPLIT, 2)
+                for s in range(0, 2, step):
+                    nc.gpsimd.tensor_tensor(
+                        out=o_sb[(h, c)][:, s : s + step, :], in0=h2w[(h, c)][:, s : s + step, :], in1=prev[:, s : s + step, :], op=ALU.add
+                    )
+
+        def do_st(h, c):
+            nc.sync.dma_start(
+                out=out[256 * c : 256 * (c + 1), 256 * h : 256 * (h + 1)].rearrange("(p e) d -> p e d", e=2),
+                in_=o_sb[(h, c)][:],
+            )
+
+        two = {"w0x": do_w0x, "h1c": do_h1c, "h1w": do_h1w, "acc": do_acc, "fin": do_fin, "h2w": do_h2w}
+        for step_name in ORDER:
+            if step_name[:3] == "xrg":
+                do_xrg(step_name[3], int(step_name[4]))
+            elif step_name[:3] == "ATc":
+                do_ATc(int(step_name[3]))
+            elif step_name[:3] in two:
+                two[step_name[:3]](int(step_name[3]), int(step_name[4]))
+            elif step_name[:2] == "xq":
+                do_xq(int(step_name[2]))
+            elif step_name[:2] == "Aq":
+                do_Aq(int(step_name[2]))
+            elif step_name[:2] == "hq":
+                do_hq(int(step_name[2]), int(step_name[3]))
+            elif step_name[:2] == "st":
+                do_st(int(step_name[2]), int(step_name[3]))
+            elif step_name[0] == "T":
+                do_T(int(step_name[1]))
+            elif step_name[0] == "M":
+                do_M(int(step_name[1]), int(step_name[3]))
+            else:
+                do_O(int(step_name[1]), int(step_name[2]))

@@ -20,24 +20,25 @@ PIN = True
 XS = 256
 GSPLIT = 1
 ATC_ENG = "SSSSSSSS"
-H1C_ENG = {(1, 0): "S", (1, 1): "S", (1, 2): "S", (1, 3): "S", (0, 0): "S", (0, 1): "S", (0, 2): "S", (0, 3): "S"}
+H1C_ENG = {(1, 0): "S", (1, 1): "V", (1, 2): "S", (1, 3): "V", (0, 0): "S", (0, 1): "S", (0, 2): "S", (0, 3): "S"}
 W0X_ENG = {(1, 0): "V", (1, 1): "V", (0, 0): "V", (0, 1): "V"}
-ACC_PATH = {(1, 0): "V", (1, 1): "V", (1, 2): "V", (1, 3): "V", (0, 0): "V", (0, 1): "V", (0, 2): "V", (0, 3): "V"}
+ACC_PATH = {(1, 0): "G", (1, 1): "G", (1, 2): "G", (1, 3): "G", (0, 0): "V", (0, 1): "V", (0, 2): "V", (0, 3): "G"}
 FIN_PATH = {(1, 0): "V", (1, 1): "V", (1, 2): "V", (1, 3): "V", (0, 0): "V", (0, 1): "V", (0, 2): "V", (0, 3): "V"}
 T_BANK = [4, 5, 6, 7, 4, 5, 6, 7]
 H_BANK = {(1, 0): 4, (1, 1): 5, (1, 2): 6, (1, 3): 7, (0, 0): 0, (0, 1): 1, (0, 2): 2, (0, 3): 3}
-O_BANK = {(1, 0): 4, (1, 1): 5, (1, 2): 6, (1, 3): 7, (0, 0): 0, (0, 1): 1, (0, 2): 2, (0, 3): 3}
+O_BANK = {(1, 0): 2, (1, 1): 3, (1, 2): 6, (1, 3): 7, (0, 0): 0, (0, 1): 1, (0, 2): 4, (0, 3): 5}
 LOADS = ["x0", "x1", "A0", "A1", "A2", "A3"]
 ORDER = [
-    "xrgV0", "xrgS0", "xrgV1", "xrgS1", "xq0", "T0", "xq1", "T1", "ATc0", "w0x00", "ATc1", "T2",
-    "T3", "ATc2", "Aq0", "ATc3", "w0x01", "T4", "T5", "ATc4", "Aq1", "M0b0", "M0b1", "M0b2",
-    "ATc5", "w0x10", "M0b3", "T6", "Aq2", "T7", "ATc6", "M1b0", "w0x11", "M1b1", "ATc7", "M1b2",
-    "M1b3", "M2b0", "M2b1", "Aq3", "M2b2", "M2b3", "M3b0", "M3b1", "h1c00", "M3b2", "M3b3", "M4b0",
-    "M4b1", "acc00", "h1c01", "M5b0", "M5b1", "M6b0", "M6b1", "h1c02", "acc01", "M7b0", "M7b1", "M4b2",
-    "h1c03", "M4b3", "hq00", "M5b2", "M5b3", "acc02", "M6b2", "h1c10", "M6b3", "M7b2", "M7b3", "acc03",
-    "h1c11", "hq01", "h1c12", "hq10", "acc10", "h1c13", "O00", "acc11", "O01", "hq11", "O02", "fin00",
-    "O03", "acc12", "st00", "O10", "fin01", "O11", "acc13", "st01", "O12", "fin02", "O13", "fin03",
-    "st02", "fin10", "st03", "fin11", "st10", "fin12", "st11", "fin13", "st12", "st13",
+    "w0x01", "xrgV0", "T0", "T1", "xrgS0", "xrgS1", "T2", "ATc0", "xq0", "ATc1", "w0x11", "w0x10",
+    "xrgV1", "xq1", "T3", "ATc2", "T4", "Aq0", "T5", "M0b2", "ATc3", "ATc4", "Aq1", "M1b3",
+    "ATc5", "T7", "T6", "M2b2", "M2b3", "M0b3", "M3b3", "ATc7", "w0x00", "Aq2", "ATc6", "M1b2",
+    "Aq3", "M3b2", "h1w03", "acc02", "h1c03", "M1b1", "M4b2", "M2b0", "M5b3", "h1c02", "M5b2", "M4b3",
+    "M6b3", "M7b3", "M0b0", "M7b2", "M6b2", "M1b0", "h1c13", "h1c12", "M3b0", "h1w12", "M5b1", "M3b1",
+    "hq01", "M2b1", "M0b1", "M6b1", "h1c01", "acc03", "acc00", "M7b1", "M4b1", "M7b0", "M6b0", "M5b0",
+    "h1w13", "M4b0", "h1c10", "hq11", "h1c11", "O10", "acc12", "h1c00", "h1w11", "acc01", "acc13", "O11",
+    "O12", "O13", "fin10", "st10", "fin11", "st11", "hq10", "acc11", "hq00", "h1w10", "O00", "fin12",
+    "st12", "acc10", "fin13", "st13", "O01", "fin00", "st00", "O03", "fin01", "st01", "O02", "fin03",
+    "st03", "fin02", "st02",
 ]
 
 

@@ -27,18 +27,19 @@ FIN_PATH = {(1, 0): "V", (1, 1): "V", (1, 2): "V", (1, 3): "V", (0, 0): "V", (0,
 T_BANK = [4, 5, 6, 7, 4, 5, 6, 7]
 H_BANK = {(1, 0): 4, (1, 1): 5, (1, 2): 6, (1, 3): 7, (0, 0): 0, (0, 1): 1, (0, 2): 2, (0, 3): 3}
 O_BANK = {(1, 0): 2, (1, 1): 3, (1, 2): 6, (1, 3): 7, (0, 0): 0, (0, 1): 1, (0, 2): 4, (0, 3): 5}
+W_BANK = 3
 LOADS = ["x0", "x1", "A0", "A1", "A2", "A3"]
 ORDER = [
-    "w0x01", "xrgV0", "T0", "T1", "xrgS0", "xrgS1", "T2", "ATc0", "xq0", "ATc1", "w0x11", "w0x10",
-    "xrgV1", "xq1", "T3", "ATc2", "T4", "Aq0", "T5", "M0b2", "ATc3", "ATc4", "Aq1", "M1b3",
-    "ATc5", "T7", "T6", "M2b2", "M2b3", "M0b3", "M3b3", "ATc7", "w0x00", "Aq2", "ATc6", "M1b2",
-    "Aq3", "M3b2", "h1w03", "acc02", "h1c03", "M1b1", "M4b2", "M2b0", "M5b3", "h1c02", "M5b2", "M4b3",
-    "M6b3", "M7b3", "M0b0", "M7b2", "M6b2", "M1b0", "h1c13", "h1c12", "M3b0", "h1w12", "M5b1", "M3b1",
-    "hq01", "M2b1", "M0b1", "M6b1", "h1c01", "acc03", "acc00", "M7b1", "M4b1", "M7b0", "M6b0", "M5b0",
-    "h1w13", "M4b0", "h1c10", "hq11", "h1c11", "O10", "acc12", "h1c00", "h1w11", "acc01", "acc13", "O11",
-    "O12", "O13", "fin10", "st10", "fin11", "st11", "hq10", "acc11", "hq00", "h1w10", "O00", "fin12",
-    "st12", "acc10", "fin13", "st13", "O01", "fin00", "st00", "O03", "fin01", "st01", "O02", "fin03",
-    "st03", "fin02", "st02",
+    "w0x01", "xrgV0", "W0", "W0", "W0", "W1", "W1", "T0", "T1", "W1", "xrgS0", "xrgS1",
+    "T2", "ATc0", "xq0", "ATc1", "w0x11", "w0x10", "xrgV1", "xq1", "T3", "W1", "ATc2", "T4",
+    "Aq0", "T5", "W1", "M0b2", "ATc3", "ATc4", "Aq1", "M1b3", "ATc5", "T7", "T6", "M2b2",
+    "M2b3", "M0b3", "M3b3", "ATc7", "w0x00", "Aq2", "ATc6", "M1b2", "Aq3", "M3b2", "h1w03", "acc02",
+    "h1c03", "M1b1", "M4b2", "M2b0", "M5b3", "h1c02", "M5b2", "M4b3", "M6b3", "M7b3", "M0b0", "M7b2",
+    "M6b2", "M1b0", "h1c13", "h1c12", "M3b0", "h1w12", "M5b1", "M3b1", "hq01", "M2b1", "M0b1", "M6b1",
+    "h1c01", "acc03", "acc00", "M7b1", "M4b1", "M7b0", "M6b0", "M5b0", "h1w13", "M4b0", "h1c10", "hq11",
+    "h1c11", "O10", "acc12", "h1c00", "h1w11", "acc01", "acc13", "O11", "O12", "O13", "fin10", "st10",
+    "fin11", "st11", "hq10", "acc11", "hq00", "h1w10", "O00", "fin12", "st12", "acc10", "fin13", "st13",
+    "O01", "fin00", "st00", "O03", "fin01", "st01", "O02", "fin03", "st03", "fin02", "st02",
 ]
 
 
@@ -254,6 +255,13 @@ def tile_simpa_pb_kernel(tc, A_p, x_p, w_p, out):
                 in_=o_sb[(h, c)][:],
             )
 
+        warm = {}
+
+        def do_W(g):
+            if 0 not in warm:
+                warm[0] = psum.tile([P, D], F32, tag="bank%d" % W_BANK, name="warm")
+            nc.tensor.matmul(out=warm[0][:], lhsT=x_sb[g][:, 0, 0:P], rhs=x_sb[g][:, 1, :], start=True, stop=True)
+
         two = {"w0x": do_w0x, "h1c": do_h1c, "h1w": do_h1w, "acc": do_acc, "fin": do_fin, "h2w": do_h2w}
         for step_name in ORDER:
             if step_name[:3] == "xrg":
@@ -270,6 +278,8 @@ def tile_simpa_pb_kernel(tc, A_p, x_p, w_p, out):
                 do_hq(int(step_name[2]), int(step_name[3]))
             elif step_name[:2] == "st":
                 do_st(int(step_name[2]), int(step_name[3]))
+            elif step_name[0] == "W":
+                do_W(int(step_name[1]))
             elif step_name[0] == "T":
                 do_T(int(step_name[1]))
             elif step_name[0] == "M":

@@ -12,35 +12,15 @@ ALU = mybir.AluOpType
 ACT = mybir.ActivationFunctionType
 
 P = 128
-N = 1024
-D = 512
-FLOPS = 2 * 2 * N * N * D
+NODES = 1024
+FEATS = 512
+PACK = 4
+HALF = FEATS // 2
+CHUNK = HALF // 2
+FLOPS = 2 * 2 * NODES * NODES * FEATS
 
-PIN = True
-XS = 256
-GSPLIT = 1
-ATC_ENG = "SSSSSSSS"
-H1C_ENG = {(1, 0): "S", (1, 1): "V", (1, 2): "S", (1, 3): "V", (0, 0): "S", (0, 1): "S", (0, 2): "S", (0, 3): "S"}
-W0X_ENG = {(1, 0): "V", (1, 1): "V", (0, 0): "V", (0, 1): "V"}
-ACC_PATH = {(1, 0): "G", (1, 1): "G", (1, 2): "G", (1, 3): "G", (0, 0): "V", (0, 1): "V", (0, 2): "V", (0, 3): "G"}
-FIN_PATH = {(1, 0): "V", (1, 1): "V", (1, 2): "V", (1, 3): "V", (0, 0): "V", (0, 1): "V", (0, 2): "V", (0, 3): "V"}
-T_BANK = [4, 5, 6, 7, 4, 5, 6, 7]
-H_BANK = {(1, 0): 4, (1, 1): 5, (1, 2): 6, (1, 3): 7, (0, 0): 0, (0, 1): 1, (0, 2): 2, (0, 3): 3}
-O_BANK = {(1, 0): 2, (1, 1): 3, (1, 2): 6, (1, 3): 7, (0, 0): 0, (0, 1): 1, (0, 2): 4, (0, 3): 5}
-W_BANK = 3
-LOADS = ["x0", "x1", "A0", "A1", "A2", "A3"]
-ORDER = [
-    "w0x01", "xrgV0", "W0", "W0", "W0", "W1", "W1", "T0", "T1", "W1", "xrgS0", "xrgS1",
-    "T2", "ATc0", "xq0", "ATc1", "w0x11", "w0x10", "xrgV1", "xq1", "T3", "W1", "ATc2", "T4",
-    "Aq0", "T5", "W1", "M0b2", "ATc3", "ATc4", "Aq1", "M1b3", "ATc5", "T7", "T6", "M2b2",
-    "M2b3", "M0b3", "M3b3", "ATc7", "w0x00", "Aq2", "ATc6", "M1b2", "Aq3", "M3b2", "h1w03", "acc02",
-    "h1c03", "M1b1", "M4b2", "M2b0", "M5b3", "h1c02", "M5b2", "M4b3", "M6b3", "M7b3", "M0b0", "M7b2",
-    "M6b2", "M1b0", "h1c13", "h1c12", "M3b0", "h1w12", "M5b1", "M3b1", "hq01", "M2b1", "M0b1", "M6b1",
-    "h1c01", "acc03", "acc00", "M7b1", "M4b1", "M7b0", "M6b0", "M5b0", "h1w13", "M4b0", "h1c10", "hq11",
-    "h1c11", "O10", "acc12", "h1c00", "h1w11", "acc01", "acc13", "O11", "O12", "O13", "fin10", "st10",
-    "fin11", "st11", "hq10", "acc11", "hq00", "h1w10", "O00", "fin12", "st12", "acc10", "fin13", "st13",
-    "O01", "fin00", "st00", "O03", "fin01", "st01", "O02", "fin03", "st03", "fin02", "st02",
-]
+X_SCALAR_COLS = 256
+GPSIMD_OUTPUTS = 3
 
 
 def tile_simpa_pb_kernel(tc, A_p, x_p, w_p, out):
@@ -48,241 +28,217 @@ def tile_simpa_pb_kernel(tc, A_p, x_p, w_p, out):
     with ExitStack() as ctx:
         keep = ctx.enter_context(tc.tile_pool(name="keep", bufs=1))
         psum = ctx.enter_context(tc.psum_pool(name="psum", bufs=1))
-        if PIN:
-            ctx.enter_context(tc.manual_schedule())
+        ctx.enter_context(tc.manual_schedule())
 
-        def copy_on(eng, dst, src):
-            if eng == "S":
-                nc.scalar.copy(out=dst, in_=src)
-            else:
-                nc.vector.tensor_copy(out=dst, in_=src)
+        def bank(number, shape, name):
+            return psum.tile(shape, F32, tag="bank%d" % number, name=name)
 
         w_bf = keep.tile([P, 3], BF16, name="w_bf")
         nc.scalar.dma_start(out=w_bf[:], in_=w_p.rearrange("a b -> (a b)").partition_broadcast(P))
-        x_sb = {}
-        a_sb = {}
-        for name in LOADS:
-            i = int(name[1])
-            if name[0] == "x":
-                xt = keep.tile([P, 4, D], BF16, name="x_sb%d" % i)
-                nc.sync.dma_start(
-                    out=xt[:].rearrange("p (u e) d -> p u (e d)", e=2),
-                    in_=x_p[512 * i : 512 * (i + 1), :].rearrange("(u p e) d -> p u (e d)", u=2, e=2),
-                )
-                x_sb[i] = xt
-            else:
-                at = keep.tile([P, 2, N], BF16, name="a_sb%d" % i)
-                nc.sync.dma_start(
-                    out=at[:].rearrange("p e j -> p (e j)"),
-                    in_=A_p[256 * i : 256 * (i + 1), :].rearrange("(p e) j -> p (e j)", e=2),
-                )
-                a_sb[i] = at
+        x_sb = []
+        for g in range(2):
+            x_rows = keep.tile([P, PACK, FEATS], BF16, name="x_sb%d" % g)
+            nc.sync.dma_start(
+                out=x_rows[:].rearrange("p (u e) d -> p u (e d)", e=2),
+                in_=x_p[512 * g : 512 * (g + 1), :].rearrange("(u p e) d -> p u (e d)", u=2, e=2),
+            )
+            x_sb.append(x_rows)
+        a_sb = []
+        for c in range(4):
+            a_rows = keep.tile([P, 2, NODES], BF16, name="a_sb%d" % c)
+            nc.sync.dma_start(
+                out=a_rows[:].rearrange("p e j -> p (e j)"),
+                in_=A_p[256 * c : 256 * (c + 1), :].rearrange("(p e) j -> p (e j)", e=2),
+            )
+            a_sb.append(a_rows)
         ident = keep.tile([P, P], F32, name="ident")
         make_identity(nc, ident[:])
         w_f = keep.tile([P, 3], F32, name="w_f")
         nc.vector.tensor_copy(out=w_f[:], in_=w_bf[:])
 
-        xg = {}
-        x_codes = {}
-        x_scales = {}
+        x_grouped = []
+        x_codes = []
+        x_scales = []
 
-        def do_xrg(eng, g):
-            if g not in xg:
-                xg[g] = keep.tile([P, D, 4], BF16, name="xg%d" % g, align_bytes=64)
-            lo, hi = (0, D - XS) if eng == "V" else (D - XS, D)
-            copy_on(
-                eng,
-                xg[g][:, lo:hi, :].rearrange("p (c i) t -> p c t i", i=4),
-                x_sb[g][:, :, lo:hi].rearrange("p t (c i) -> p c t i", i=4),
-            )
+        def regroup_x(g):
+            grouped = keep.tile([P, FEATS, PACK], BF16, name="x_grouped%d" % g, align_bytes=64)
+            split = FEATS - X_SCALAR_COLS
+            for copy, lo, hi in ((nc.vector.tensor_copy, 0, split), (nc.scalar.copy, split, FEATS)):
+                copy(
+                    out=grouped[:, lo:hi, :].rearrange("p (c i) t -> p c t i", i=4),
+                    in_=x_sb[g][:, :, lo:hi].rearrange("p t (c i) -> p c t i", i=4),
+                )
+            x_grouped.append(grouped)
 
-        def do_xq(g):
-            x_codes[g] = keep.tile([P, D], U32, name="x_codes%d" % g, align_bytes=64)
-            x_scales[g] = keep.tile([P, D], U8, name="x_scales%d" % g, align_bytes=64)
+        def quantise_x(g):
+            codes = keep.tile([P, FEATS], U32, name="x_codes%d" % g, align_bytes=64)
+            scales = keep.tile([P, FEATS], U8, name="x_scales%d" % g, align_bytes=64)
             nc.vector.quantize_mx(
-                out=x_codes[g][:].bitcast(FP8X4), scales=x_scales[g][:], in_=xg[g][:].rearrange("p d t -> p (d t)")
+                out=codes[:].bitcast(FP8X4), scales=scales[:], in_=x_grouped[g][:].rearrange("p d t -> p (d t)")
+            )
+            x_codes.append(codes)
+            x_scales.append(scales)
+
+        w0_x = {}
+
+        def scale_x(g, half):
+            w0_x[(g, half)] = keep.tile([P, PACK, HALF], F32, name="w0_x%d%d" % (g, half))
+            nc.vector.tensor_scalar(
+                out=w0_x[(g, half)][:],
+                in0=x_sb[g][:, :, HALF * half : HALF * (half + 1)],
+                scalar1=w_f[:, 0:1],
+                scalar2=None,
+                op0=ALU.mult,
             )
 
-        w0x = {}
-
-        def do_w0x(g, h):
-            t = keep.tile([P, 4, 256], F32, name="w0x%d%d" % (g, h))
-            src = x_sb[g][:, :, 256 * h : 256 * (h + 1)]
-            if W0X_ENG[(g, h)] == "S":
-                nc.scalar.activation(out=t[:], in_=src, func=ACT.Copy, scale=w_f[:, 0:1])
-            elif W0X_ENG[(g, h)] == "V":
-                nc.vector.tensor_scalar(out=t[:], in0=src, scalar1=w_f[:, 0:1], scalar2=None, op0=ALU.mult)
-            else:
-                nc.gpsimd.tensor_scalar(out=t[:], in0=src, scalar1=w_f[:, 0:1], scalar2=0.0, op0=ALU.mult, op1=ALU.add)
-            w0x[(g, h)] = t
-
-        tp = {}
-        ag = {}
+        a_t = {}
+        a_grouped = {}
         a_codes = {}
         a_scales = {}
 
-        def do_T(m):
-            c, e = divmod(m, 2)
-            t = psum.tile([P, 4, P], F32, tag="bank%d" % T_BANK[m], name="tp%d" % m)
-            aw = a_sb[c][:, e, :].bitcast(F32)
+        def transpose_tile(m):
+            a_t[m] = bank(4 + m % 4, [P, 4, P], "a_t%d" % m)
+            words = a_sb[m // 2][:, m % 2, :].bitcast(F32)
             for k in range(4):
-                nc.tensor.transpose(t[:, k, :], aw[:, P * k : P * (k + 1)], ident[:])
-            tp[m] = t
+                nc.tensor.transpose(a_t[m][:, k, :], words[:, P * k : P * (k + 1)], ident[:])
 
-        def do_ATc(m):
-            c, e = divmod(m, 2)
-            if c not in ag:
-                ag[c] = keep.tile([P, 2, N], BF16, name="ag%d" % c, align_bytes=64)
-            copy_on(
-                ATC_ENG[m],
-                ag[c][:, e, :].bitcast(F32).rearrange("p (g i u) -> p g i u", g=2, u=2),
-                tp[m][:].rearrange("p (g u) i -> p g i u", u=2),
+        def copy_tile(m):
+            if m % 2 == 0:
+                a_grouped[m // 2] = keep.tile([P, 2, NODES], BF16, name="a_grouped%d" % (m // 2), align_bytes=64)
+            nc.scalar.copy(
+                out=a_grouped[m // 2][:, m % 2, :].bitcast(F32).rearrange("p (g i u) -> p g i u", g=2, u=2),
+                in_=a_t[m][:].rearrange("p (g u) i -> p g i u", u=2),
             )
 
-        def do_Aq(c):
-            a_codes[c] = keep.tile([P, 512], U32, name="a_codes%d" % c, align_bytes=64)
-            a_scales[c] = keep.tile([P, 512], U8, name="a_scales%d" % c, align_bytes=64)
+        def quantise_pair(c):
+            a_codes[c] = keep.tile([P, 4 * P], U32, name="a_codes%d" % c, align_bytes=64)
+            a_scales[c] = keep.tile([P, 4 * P], U8, name="a_scales%d" % c, align_bytes=64)
             nc.vector.quantize_mx(
-                out=a_codes[c][:].bitcast(FP8X4), scales=a_scales[c][:], in_=ag[c][:].rearrange("p e k -> p (e k)")
+                out=a_codes[c][:].bitcast(FP8X4),
+                scales=a_scales[c][:],
+                in_=a_grouped[c][:].rearrange("p e k -> p (e k)"),
             )
 
-        def lhs(m, gp):
-            c, e = divmod(m, 2)
-            lo = (2 * e + gp) * P
-            return a_codes[c][:, lo : lo + P].bitcast(FP8X4), a_scales[c][:, lo : lo + P]
-
-        hb = {}
-
-        def do_M(m, b):
-            g, t = divmod(m, 4)
-            if (g, b) not in hb:
-                hb[(g, b)] = psum.tile([P, 4, P], F32, tag="bank%d" % H_BANK[(g, b)], name="hb%d%d" % (g, b))
-            for gp in range(2):
-                lt, ls = lhs(m, gp)
+        def multiply(acc, m, moving_codes, moving_scales):
+            for g in range(2):
+                lo = (2 * (m % 2) + g) * P
                 nc.tensor.matmul_mx(
-                    out=hb[(g, b)][:, t, :],
-                    lhsT=lt,
-                    lhsT_scale=ls,
-                    rhs=x_codes[gp][:, P * b : P * (b + 1)].bitcast(FP8X4),
-                    rhs_scale=x_scales[gp][:, P * b : P * (b + 1)],
-                    start=(gp == 0),
-                    stop=(gp == 1),
+                    out=acc,
+                    lhsT=a_codes[m // 2][:, lo : lo + P].bitcast(FP8X4),
+                    lhsT_scale=a_scales[m // 2][:, lo : lo + P],
+                    rhs=moving_codes[g].bitcast(FP8X4),
+                    rhs_scale=moving_scales[g],
+                    start=(g == 0),
+                    stop=(g == 1),
                 )
 
-        hg = {}
-        acc = {}
-        h1w = {}
+        h1 = {}
+
+        def first_product(m, half):
+            g, t = divmod(m, PACK)
+            for r in range(2):
+                if t == 0:
+                    h1[(g, half, r)] = bank(4 * half + 2 * g + r, [P, PACK, CHUNK], "h1_%d%d%d" % (g, half, r))
+                cols = slice(HALF * half + CHUNK * r, HALF * half + CHUNK * (r + 1))
+                multiply(h1[(g, half, r)][:, t, :], m, [c[:, cols] for c in x_codes], [s[:, cols] for s in x_scales])
+
+        partial = {}
         h_codes = {}
         h_scales = {}
 
-        def do_h1c(g, b):
-            h, r = divmod(b, 2)
-            if (g, h) not in hg:
-                hg[(g, h)] = keep.tile([P, 256, 4], BF16, name="hg%d%d" % (g, h), align_bytes=64)
-            copy_on(H1C_ENG[(g, b)], hg[(g, h)][:, P * r : P * (r + 1), :], hb[(g, b)][:].rearrange("p t d -> p d t"))
+        def add_h1(g, half, r):
+            cols = slice(CHUNK * r, CHUNK * (r + 1))
+            nc.vector.scalar_tensor_tensor(
+                out=partial[(g, half)][:, :, cols],
+                in0=h1[(g, half, r)][:],
+                scalar=w_f[:, 1:2],
+                in1=w0_x[(g, half)][:, :, cols],
+                op0=ALU.mult,
+                op1=ALU.add,
+            )
 
-        def do_h1w(g, b):
-            h1w[(g, b)] = keep.tile([P, 4, P], F32, name="h1w%d%d" % (g, b))
-            nc.scalar.activation(out=h1w[(g, b)][:], in_=hb[(g, b)][:], func=ACT.Copy, scale=w_f[:, 1:2])
-
-        def do_acc(g, b):
-            h, r = divmod(b, 2)
-            if (g, h) not in acc:
-                acc[(g, h)] = keep.tile([P, 4, 256], F32, name="acc%d%d" % (g, h))
-            dst = acc[(g, h)][:, :, P * r : P * (r + 1)]
-            prev = w0x[(g, h)][:, :, P * r : P * (r + 1)]
-            if ACC_PATH[(g, b)] == "V":
-                nc.vector.scalar_tensor_tensor(
-                    out=dst, in0=hb[(g, b)][:], scalar=w_f[:, 1:2], in1=prev, op0=ALU.mult, op1=ALU.add
+        def drain(g, half):
+            grouped = keep.tile([P, HALF, PACK], BF16, name="h_grouped%d%d" % (g, half), align_bytes=64)
+            partial[(g, half)] = keep.tile([P, PACK, HALF], F32, name="partial%d%d" % (g, half))
+            h_codes[(g, half)] = keep.tile([P, HALF], U32, name="h_codes%d%d" % (g, half), align_bytes=64)
+            h_scales[(g, half)] = keep.tile([P, HALF], U8, name="h_scales%d%d" % (g, half), align_bytes=64)
+            for r in range(2):
+                nc.scalar.copy(
+                    out=grouped[:, CHUNK * r : CHUNK * (r + 1), :], in_=h1[(g, half, r)][:].rearrange("p t d -> p d t")
                 )
-            else:
-                step = 4 // GSPLIT
-                for s in range(0, 4, step):
-                    nc.gpsimd.tensor_tensor(
-                        out=dst[:, s : s + step, :], in0=h1w[(g, b)][:, s : s + step, :], in1=prev[:, s : s + step, :], op=ALU.add
-                    )
-
-        def do_hq(g, h):
-            h_codes[(g, h)] = keep.tile([P, 256], U32, name="h_codes%d%d" % (g, h), align_bytes=64)
-            h_scales[(g, h)] = keep.tile([P, 256], U8, name="h_scales%d%d" % (g, h), align_bytes=64)
+            add_h1(g, half, 0)
             nc.vector.quantize_mx(
-                out=h_codes[(g, h)][:].bitcast(FP8X4),
-                scales=h_scales[(g, h)][:],
-                in_=hg[(g, h)][:].rearrange("p d t -> p (d t)"),
+                out=h_codes[(g, half)][:].bitcast(FP8X4),
+                scales=h_scales[(g, half)][:],
+                in_=grouped[:].rearrange("p d t -> p (d t)"),
             )
+            add_h1(g, half, 1)
 
-        ob = {}
-        h2w = {}
-        o_sb = {}
+        h2 = {}
+        result = {}
 
-        def do_O(h, c):
-            ob[(h, c)] = psum.tile([P, 2, 256], F32, tag="bank%d" % O_BANK[(h, c)], name="ob%d%d" % (h, c))
+        def second_product(half, c):
+            h2[(half, c)] = bank(4 * half + c, [P, 2, HALF], "h2_%d%d" % (half, c))
+            result[(half, c)] = keep.tile([P, 2, HALF], F32, name="result%d%d" % (half, c))
             for e in range(2):
-                for gp in range(2):
-                    lt, ls = lhs(2 * c + e, gp)
-                    nc.tensor.matmul_mx(
-                        out=ob[(h, c)][:, e, :],
-                        lhsT=lt,
-                        lhsT_scale=ls,
-                        rhs=h_codes[(gp, h)][:].bitcast(FP8X4),
-                        rhs_scale=h_scales[(gp, h)][:],
-                        start=(gp == 0),
-                        stop=(gp == 1),
-                    )
-
-        def do_h2w(h, c):
-            h2w[(h, c)] = keep.tile([P, 2, 256], F32, name="h2w%d%d" % (h, c))
-            nc.scalar.activation(out=h2w[(h, c)][:], in_=ob[(h, c)][:], func=ACT.Copy, scale=w_f[:, 2:3])
-
-        def do_fin(h, c):
-            g, u = divmod(c, 2)
-            o_sb[(h, c)] = keep.tile([P, 2, 256], F32, name="o%d%d" % (h, c))
-            prev = acc[(g, h)][:, 2 * u : 2 * u + 2, :]
-            if FIN_PATH[(h, c)] == "V":
-                nc.vector.scalar_tensor_tensor(
-                    out=o_sb[(h, c)][:], in0=ob[(h, c)][:], scalar=w_f[:, 2:3], in1=prev, op0=ALU.mult, op1=ALU.add
+                multiply(
+                    h2[(half, c)][:, e, :],
+                    2 * c + e,
+                    [h_codes[(g, half)][:] for g in range(2)],
+                    [h_scales[(g, half)][:] for g in range(2)],
                 )
-            else:
-                step = 2 // min(GSPLIT, 2)
-                for s in range(0, 2, step):
-                    nc.gpsimd.tensor_tensor(
-                        out=o_sb[(h, c)][:, s : s + step, :], in0=h2w[(h, c)][:, s : s + step, :], in1=prev[:, s : s + step, :], op=ALU.add
-                    )
 
-        def do_st(h, c):
-            nc.sync.dma_start(
-                out=out[256 * c : 256 * (c + 1), 256 * h : 256 * (h + 1)].rearrange("(p e) d -> p e d", e=2),
-                in_=o_sb[(h, c)][:],
+        def earlier_terms(half, c):
+            return partial[(c // 2, half)][:, 2 * (c % 2) : 2 * (c % 2) + 2, :]
+
+        def store(queue, half, c):
+            queue.dma_start(
+                out=out[256 * c : 256 * (c + 1), HALF * half : HALF * (half + 1)].rearrange("(p e) d -> p e d", e=2),
+                in_=result[(half, c)][:],
             )
 
-        warm = {}
+        for g in range(2):
+            regroup_x(g)
+        for g in range(2):
+            quantise_x(g)
+        for c in range(4):
+            for m in (2 * c, 2 * c + 1):
+                transpose_tile(m)
+            for m in (2 * c, 2 * c + 1):
+                copy_tile(m)
+            scale_x(c % 2, c // 2)
+            quantise_pair(c)
+            if c >= 2:
+                for m in (2 * c - 4, 2 * c - 3):
+                    first_product(m, 0)
+        for m in range(4, 8):
+            first_product(m, 0)
+        for g in range(2):
+            drain(g, 0)
+        for m in range(8):
+            first_product(m, 1)
+        for g in range(2):
+            drain(g, 1)
 
-        def do_W(g):
-            if 0 not in warm:
-                warm[0] = psum.tile([P, D], F32, tag="bank%d" % W_BANK, name="warm")
-            nc.tensor.matmul(out=warm[0][:], lhsT=x_sb[g][:, 0, 0:P], rhs=x_sb[g][:, 1, :], start=True, stop=True)
-
-        two = {"w0x": do_w0x, "h1c": do_h1c, "h1w": do_h1w, "acc": do_acc, "fin": do_fin, "h2w": do_h2w}
-        for step_name in ORDER:
-            if step_name[:3] == "xrg":
-                do_xrg(step_name[3], int(step_name[4]))
-            elif step_name[:3] == "ATc":
-                do_ATc(int(step_name[3]))
-            elif step_name[:3] in two:
-                two[step_name[:3]](int(step_name[3]), int(step_name[4]))
-            elif step_name[:2] == "xq":
-                do_xq(int(step_name[2]))
-            elif step_name[:2] == "Aq":
-                do_Aq(int(step_name[2]))
-            elif step_name[:2] == "hq":
-                do_hq(int(step_name[2]), int(step_name[3]))
-            elif step_name[:2] == "st":
-                do_st(int(step_name[2]), int(step_name[3]))
-            elif step_name[0] == "W":
-                do_W(int(step_name[1]))
-            elif step_name[0] == "T":
-                do_T(int(step_name[1]))
-            elif step_name[0] == "M":
-                do_M(int(step_name[1]), int(step_name[3]))
-            else:
-                do_O(int(step_name[1]), int(step_name[2]))
+        blocks = [(half, c) for half in range(2) for c in range(4)]
+        scaled = {}
+        for half, c in blocks[:GPSIMD_OUTPUTS]:
+            second_product(half, c)
+            scaled[(half, c)] = keep.tile([P, 2, HALF], F32, name="scaled%d%d" % (half, c))
+            nc.scalar.activation(out=scaled[(half, c)][:], in_=h2[(half, c)][:], func=ACT.Copy, scale=w_f[:, 2:3])
+        for half, c in blocks[:GPSIMD_OUTPUTS]:
+            nc.gpsimd.tensor_tensor(
+                out=result[(half, c)][:], in0=scaled[(half, c)][:], in1=earlier_terms(half, c), op=ALU.add
+            )
+            store(nc.scalar, half, c)
+        for half, c in blocks[GPSIMD_OUTPUTS:]:
+            second_product(half, c)
+            nc.vector.scalar_tensor_tensor(
+                out=result[(half, c)][:],
+                in0=h2[(half, c)][:],
+                scalar=w_f[:, 2:3],
+                in1=earlier_terms(half, c),
+                op0=ALU.mult,
+                op1=ALU.add,
+            )
+            store(nc.sync, half, c)

@@ -15,12 +15,14 @@ P = 128
 NODES = 1024
 FEATS = 512
 PACK = 4
+PASSES = NODES // (P * PACK)
+PAIRS = NODES // (2 * P)
 HALF = FEATS // 2
 CHUNK = HALF // 2
 FLOPS = 2 * 2 * NODES * NODES * FEATS
 
-X_SCALAR_COLS = 256
-GPSIMD_OUTPUTS = 3
+X_SCALAR_COLS = FEATS // 2
+LAG = 2
 
 
 def tile_simpa_pb_kernel(tc, A_p, x_p, w_p, out):
@@ -36,7 +38,7 @@ def tile_simpa_pb_kernel(tc, A_p, x_p, w_p, out):
         w_bf = keep.tile([P, 3], BF16, name="w_bf")
         nc.scalar.dma_start(out=w_bf[:], in_=w_p.rearrange("a b -> (a b)").partition_broadcast(P))
         x_sb = []
-        for g in range(2):
+        for g in range(PASSES):
             x_rows = keep.tile([P, PACK, FEATS], BF16, name="x_sb%d" % g)
             nc.sync.dma_start(
                 out=x_rows[:].rearrange("p (u e) d -> p u (e d)", e=2),
@@ -44,7 +46,7 @@ def tile_simpa_pb_kernel(tc, A_p, x_p, w_p, out):
             )
             x_sb.append(x_rows)
         a_sb = []
-        for c in range(4):
+        for c in range(PAIRS):
             a_rows = keep.tile([P, 2, NODES], BF16, name="a_sb%d" % c)
             nc.sync.dma_start(
                 out=a_rows[:].rearrange("p e j -> p (e j)"),
@@ -99,37 +101,37 @@ def tile_simpa_pb_kernel(tc, A_p, x_p, w_p, out):
         def transpose_tile(m):
             a_t[m] = bank(4 + m % 4, [P, 4, P], "a_t%d" % m)
             words = a_sb[m // 2][:, m % 2, :].bitcast(F32)
-            for k in range(4):
-                nc.tensor.transpose(a_t[m][:, k, :], words[:, P * k : P * (k + 1)], ident[:])
+            for plane in range(4):
+                nc.tensor.transpose(a_t[m][:, plane, :], words[:, P * plane : P * (plane + 1)], ident[:])
 
         def copy_tile(m):
             if m % 2 == 0:
                 a_grouped[m // 2] = keep.tile([P, 2, NODES], BF16, name="a_grouped%d" % (m // 2), align_bytes=64)
             nc.scalar.copy(
-                out=a_grouped[m // 2][:, m % 2, :].bitcast(F32).rearrange("p (g i u) -> p g i u", g=2, u=2),
+                out=a_grouped[m // 2][:, m % 2, :].bitcast(F32).rearrange("p (g i u) -> p g i u", g=PASSES, u=2),
                 in_=a_t[m][:].rearrange("p (g u) i -> p g i u", u=2),
             )
 
         def quantise_pair(c):
-            a_codes[c] = keep.tile([P, 4 * P], U32, name="a_codes%d" % c, align_bytes=64)
-            a_scales[c] = keep.tile([P, 4 * P], U8, name="a_scales%d" % c, align_bytes=64)
+            a_codes[c] = keep.tile([P, 2 * PASSES * P], U32, name="a_codes%d" % c, align_bytes=64)
+            a_scales[c] = keep.tile([P, 2 * PASSES * P], U8, name="a_scales%d" % c, align_bytes=64)
             nc.vector.quantize_mx(
                 out=a_codes[c][:].bitcast(FP8X4),
                 scales=a_scales[c][:],
                 in_=a_grouped[c][:].rearrange("p e k -> p (e k)"),
             )
 
-        def multiply(acc, m, moving_codes, moving_scales):
-            for g in range(2):
-                lo = (2 * (m % 2) + g) * P
+        def multiply(group, m, moving_codes, moving_scales):
+            for g in range(PASSES):
+                lo = (PASSES * (m % 2) + g) * P
                 nc.tensor.matmul_mx(
-                    out=acc,
+                    out=group,
                     lhsT=a_codes[m // 2][:, lo : lo + P].bitcast(FP8X4),
                     lhsT_scale=a_scales[m // 2][:, lo : lo + P],
                     rhs=moving_codes[g].bitcast(FP8X4),
                     rhs_scale=moving_scales[g],
                     start=(g == 0),
-                    stop=(g == 1),
+                    stop=(g == PASSES - 1),
                 )
 
         h1 = {}
@@ -146,99 +148,94 @@ def tile_simpa_pb_kernel(tc, A_p, x_p, w_p, out):
         h_codes = {}
         h_scales = {}
 
-        def add_h1(g, half, r):
-            cols = slice(CHUNK * r, CHUNK * (r + 1))
-            nc.vector.scalar_tensor_tensor(
-                out=partial[(g, half)][:, :, cols],
-                in0=h1[(g, half, r)][:],
-                scalar=w_f[:, 1:2],
-                in1=w0_x[(g, half)][:, :, cols],
-                op0=ALU.mult,
-                op1=ALU.add,
-            )
-
-        def drain(g, half):
+        def empty_h1(g, half, adds_on_gpsimd):
             grouped = keep.tile([P, HALF, PACK], BF16, name="h_grouped%d%d" % (g, half), align_bytes=64)
             partial[(g, half)] = keep.tile([P, PACK, HALF], F32, name="partial%d%d" % (g, half))
             h_codes[(g, half)] = keep.tile([P, HALF], U32, name="h_codes%d%d" % (g, half), align_bytes=64)
             h_scales[(g, half)] = keep.tile([P, HALF], U8, name="h_scales%d%d" % (g, half), align_bytes=64)
-            for r in range(2):
-                nc.scalar.copy(
-                    out=grouped[:, CHUNK * r : CHUNK * (r + 1), :], in_=h1[(g, half, r)][:].rearrange("p t d -> p d t")
-                )
-            add_h1(g, half, 0)
-            nc.vector.quantize_mx(
-                out=h_codes[(g, half)][:].bitcast(FP8X4),
-                scales=h_scales[(g, half)][:],
-                in_=grouped[:].rearrange("p d t -> p (d t)"),
-            )
-            add_h1(g, half, 1)
+            chunks = [slice(CHUNK * r, CHUNK * (r + 1)) for r in range(2)]
 
-        h2 = {}
-        result = {}
+            def quantise_h1():
+                nc.vector.quantize_mx(
+                    out=h_codes[(g, half)][:].bitcast(FP8X4),
+                    scales=h_scales[(g, half)][:],
+                    in_=grouped[:].rearrange("p d t -> p (d t)"),
+                )
+
+            def add_on_vector(r):
+                nc.vector.scalar_tensor_tensor(
+                    out=partial[(g, half)][:, :, chunks[r]],
+                    in0=h1[(g, half, r)][:],
+                    scalar=w_f[:, 1:2],
+                    in1=w0_x[(g, half)][:, :, chunks[r]],
+                    op0=ALU.mult,
+                    op1=ALU.add,
+                )
+
+            for r in range(2):
+                nc.scalar.copy(out=grouped[:, chunks[r], :], in_=h1[(g, half, r)][:].rearrange("p t d -> p d t"))
+            if adds_on_gpsimd:
+                quantise_h1()
+                w1_h1 = keep.tile([P, 2, PACK, CHUNK], F32, name="w1_h1")
+                for r in range(2):
+                    nc.scalar.activation(out=w1_h1[:, r], in_=h1[(g, half, r)][:], func=ACT.Copy, scale=w_f[:, 1:2])
+                for r in range(2):
+                    nc.gpsimd.tensor_tensor(
+                        out=partial[(g, half)][:, :, chunks[r]],
+                        in0=w1_h1[:, r],
+                        in1=w0_x[(g, half)][:, :, chunks[r]],
+                        op=ALU.add,
+                    )
+            else:
+                add_on_vector(0)
+                quantise_h1()
+                add_on_vector(1)
 
         def second_product(half, c):
-            h2[(half, c)] = bank(4 * half + c, [P, 2, HALF], "h2_%d%d" % (half, c))
-            result[(half, c)] = keep.tile([P, 2, HALF], F32, name="result%d%d" % (half, c))
+            h2 = bank(4 * half + c, [P, 2, HALF], "h2_%d%d" % (half, c))
             for e in range(2):
                 multiply(
-                    h2[(half, c)][:, e, :],
+                    h2[:, e, :],
                     2 * c + e,
-                    [h_codes[(g, half)][:] for g in range(2)],
-                    [h_scales[(g, half)][:] for g in range(2)],
+                    [h_codes[(g, half)][:] for g in range(PASSES)],
+                    [h_scales[(g, half)][:] for g in range(PASSES)],
                 )
-
-        def earlier_terms(half, c):
-            return partial[(c // 2, half)][:, 2 * (c % 2) : 2 * (c % 2) + 2, :]
-
-        def store(queue, half, c):
-            queue.dma_start(
+            result = keep.tile([P, 2, HALF], F32, name="result%d%d" % (half, c))
+            nc.vector.scalar_tensor_tensor(
+                out=result[:],
+                in0=h2[:],
+                scalar=w_f[:, 2:3],
+                in1=partial[(c // 2, half)][:, 2 * (c % 2) : 2 * (c % 2) + 2, :],
+                op0=ALU.mult,
+                op1=ALU.add,
+            )
+            nc.sync.dma_start(
                 out=out[256 * c : 256 * (c + 1), HALF * half : HALF * (half + 1)].rearrange("(p e) d -> p e d", e=2),
-                in_=result[(half, c)][:],
+                in_=result[:],
             )
 
-        for g in range(2):
+        for g in range(PASSES):
             regroup_x(g)
-        for g in range(2):
+        for g in range(PASSES):
             quantise_x(g)
-        for c in range(4):
+        for c in range(PAIRS):
             for m in (2 * c, 2 * c + 1):
                 transpose_tile(m)
             for m in (2 * c, 2 * c + 1):
                 copy_tile(m)
             scale_x(c % 2, c // 2)
             quantise_pair(c)
-            if c >= 2:
-                for m in (2 * c - 4, 2 * c - 3):
+            if c >= LAG:
+                for m in (2 * (c - LAG), 2 * (c - LAG) + 1):
                     first_product(m, 0)
-        for m in range(4, 8):
+        for m in range(2 * (PAIRS - LAG), 2 * PAIRS):
             first_product(m, 0)
-        for g in range(2):
-            drain(g, 0)
-        for m in range(8):
+        for g in range(PASSES):
+            empty_h1(g, 0, adds_on_gpsimd=False)
+        for m in range(2 * PAIRS):
             first_product(m, 1)
-        for g in range(2):
-            drain(g, 1)
-
-        blocks = [(half, c) for half in range(2) for c in range(4)]
-        scaled = {}
-        for half, c in blocks[:GPSIMD_OUTPUTS]:
-            second_product(half, c)
-            scaled[(half, c)] = keep.tile([P, 2, HALF], F32, name="scaled%d%d" % (half, c))
-            nc.scalar.activation(out=scaled[(half, c)][:], in_=h2[(half, c)][:], func=ACT.Copy, scale=w_f[:, 2:3])
-        for half, c in blocks[:GPSIMD_OUTPUTS]:
-            nc.gpsimd.tensor_tensor(
-                out=result[(half, c)][:], in0=scaled[(half, c)][:], in1=earlier_terms(half, c), op=ALU.add
-            )
-            store(nc.scalar, half, c)
-        for half, c in blocks[GPSIMD_OUTPUTS:]:
-            second_product(half, c)
-            nc.vector.scalar_tensor_tensor(
-                out=result[(half, c)][:],
-                in0=h2[(half, c)][:],
-                scalar=w_f[:, 2:3],
-                in1=earlier_terms(half, c),
-                op0=ALU.mult,
-                op1=ALU.add,
-            )
-            store(nc.sync, half, c)
+        empty_h1(0, 1, adds_on_gpsimd=False)
+        empty_h1(1, 1, adds_on_gpsimd=True)
+        for half in range(2):
+            for c in range(PAIRS):
+                second_product(half, c)

@@ -22,7 +22,6 @@ CHUNK = HALF // 2
 FLOPS = 2 * 2 * NODES * NODES * FEATS
 
 X_SCALAR_COLS = FEATS // 2
-LAG = 2
 
 
 def tile_simpa_pb_kernel(tc, A_p, x_p, w_p, out):
@@ -99,7 +98,7 @@ def tile_simpa_pb_kernel(tc, A_p, x_p, w_p, out):
         a_scales = {}
 
         def transpose_tile(m):
-            a_t[m] = bank(4 + m % 4, [P, 4, P], "a_t%d" % m)
+            a_t[m] = bank(m, [P, 4, P], "a_t%d" % m)
             words = a_sb[m // 2][:, m % 2, :].bitcast(F32)
             for plane in range(4):
                 nc.tensor.transpose(a_t[m][:, plane, :], words[:, P * plane : P * (plane + 1)], ident[:])
@@ -214,8 +213,10 @@ def tile_simpa_pb_kernel(tc, A_p, x_p, w_p, out):
                 in_=result[:],
             )
 
-        for g in range(PASSES):
-            regroup_x(g)
+        regroup_x(0)
+        for half in range(2):
+            scale_x(0, half)
+        regroup_x(1)
         for g in range(PASSES):
             quantise_x(g)
         for c in range(PAIRS):
@@ -223,16 +224,19 @@ def tile_simpa_pb_kernel(tc, A_p, x_p, w_p, out):
                 transpose_tile(m)
             for m in (2 * c, 2 * c + 1):
                 copy_tile(m)
-            scale_x(c % 2, c // 2)
             quantise_pair(c)
-            if c >= LAG:
-                for m in (2 * (c - LAG), 2 * (c - LAG) + 1):
-                    first_product(m, 0)
-        for m in range(2 * (PAIRS - LAG), 2 * PAIRS):
+            if c < 2:
+                scale_x(1, c)
+        last_pair = (2 * PAIRS - 2, 2 * PAIRS - 1)
+        for m in range(last_pair[0]):
+            first_product(m, 0)
+        for m in range(2):
+            first_product(m, 1)
+        for m in last_pair:
             first_product(m, 0)
         for g in range(PASSES):
             empty_h1(g, 0, adds_on_gpsimd=False)
-        for m in range(2 * PAIRS):
+        for m in range(2, 2 * PAIRS):
             first_product(m, 1)
         empty_h1(0, 1, adds_on_gpsimd=False)
         empty_h1(1, 1, adds_on_gpsimd=True)

@@ -22,6 +22,7 @@ CHUNK = HALF // 2
 FLOPS = 2 * 2 * NODES * NODES * FEATS
 
 X_SCALAR_COLS = FEATS // 2
+GPSIMD_CHUNKS = {(0, 0): (1,), (1, 0): (), (0, 1): (), (1, 1): (0, 1)}
 
 
 def tile_simpa_pb_kernel(tc, A_p, x_p, w_p, out):
@@ -147,7 +148,7 @@ def tile_simpa_pb_kernel(tc, A_p, x_p, w_p, out):
         h_codes = {}
         h_scales = {}
 
-        def empty_h1(g, half, adds_on_gpsimd):
+        def empty_h1(g, half):
             grouped = keep.tile([P, HALF, PACK], BF16, name="h_grouped%d%d" % (g, half), align_bytes=64)
             partial[(g, half)] = keep.tile([P, PACK, HALF], F32, name="partial%d%d" % (g, half))
             h_codes[(g, half)] = keep.tile([P, HALF], U32, name="h_codes%d%d" % (g, half), align_bytes=64)
@@ -173,22 +174,23 @@ def tile_simpa_pb_kernel(tc, A_p, x_p, w_p, out):
 
             for r in range(2):
                 nc.scalar.copy(out=grouped[:, chunks[r], :], in_=h1[(g, half, r)][:].rearrange("p t d -> p d t"))
-            if adds_on_gpsimd:
-                quantise_h1()
-                w1_h1 = keep.tile([P, 2, PACK, CHUNK], F32, name="w1_h1")
-                for r in range(2):
-                    nc.scalar.activation(out=w1_h1[:, r], in_=h1[(g, half, r)][:], func=ACT.Copy, scale=w_f[:, 1:2])
-                for r in range(2):
-                    nc.gpsimd.tensor_tensor(
-                        out=partial[(g, half)][:, :, chunks[r]],
-                        in0=w1_h1[:, r],
-                        in1=w0_x[(g, half)][:, :, chunks[r]],
-                        op=ALU.add,
-                    )
-            else:
-                add_on_vector(0)
-                quantise_h1()
-                add_on_vector(1)
+            vector_chunks = [r for r in range(2) if r not in GPSIMD_CHUNKS[(g, half)]]
+            for r in vector_chunks[:1]:
+                add_on_vector(r)
+            quantise_h1()
+            for r in vector_chunks[1:]:
+                add_on_vector(r)
+            if GPSIMD_CHUNKS[(g, half)]:
+                w1_h1 = keep.tile([P, 2, PACK, CHUNK], F32, name="w1_h1_%d%d" % (g, half))
+            for r in GPSIMD_CHUNKS[(g, half)]:
+                nc.scalar.activation(out=w1_h1[:, r], in_=h1[(g, half, r)][:], func=ACT.Copy, scale=w_f[:, 1:2])
+            for r in GPSIMD_CHUNKS[(g, half)]:
+                nc.gpsimd.tensor_tensor(
+                    out=partial[(g, half)][:, :, chunks[r]],
+                    in0=w1_h1[:, r],
+                    in1=w0_x[(g, half)][:, :, chunks[r]],
+                    op=ALU.add,
+                )
 
         def second_product(half, c):
             h2 = bank(4 * half + c, [P, 2, HALF], "h2_%d%d" % (half, c))
@@ -235,11 +237,11 @@ def tile_simpa_pb_kernel(tc, A_p, x_p, w_p, out):
         for m in last_pair:
             first_product(m, 0)
         for g in range(PASSES):
-            empty_h1(g, 0, adds_on_gpsimd=False)
+            empty_h1(g, 0)
         for m in range(2, 2 * PAIRS):
             first_product(m, 1)
-        empty_h1(0, 1, adds_on_gpsimd=False)
-        empty_h1(1, 1, adds_on_gpsimd=True)
+        for g in range(PASSES):
+            empty_h1(g, 1)
         for half in range(2):
             for c in range(PAIRS):
                 second_product(half, c)

from contextlib import ExitStack

import concourse.mybir as mybir
from concourse.masks import make_identity

F32 = mybir.dt.float32
BF16 = mybir.dt.bfloat16
U32 = mybir.dt.uint32
U8 = mybir.dt.uint8
FP8X4 = mybir.dt.float8_e4m3fn_x4
ALU = mybir.AluOpType
ACT = mybir.ActivationFunctionType

P = 128
NODES = 1024
FEATS = 512
PACK = 4
PASSES = NODES // (P * PACK)
PAIRS = NODES // (2 * P)
HALF = FEATS // 2
CHUNK = HALF // 2
FLOPS = 2 * 2 * NODES * NODES * FEATS

X_SCALAR_COLS = FEATS // 2
GPSIMD_CHUNKS = {(0, 0): (1,), (1, 0): (), (0, 1): (), (1, 1): (0, 1)}


def tile_simpa_pb_kernel(tc, A_p, x_p, w_p, out):
    nc = tc.nc
    with ExitStack() as ctx:
        keep = ctx.enter_context(tc.tile_pool(name="keep", bufs=1))
        psum = ctx.enter_context(tc.psum_pool(name="psum", bufs=1))
        ctx.enter_context(tc.manual_schedule())

        def bank(number, shape, name):
            return psum.tile(shape, F32, tag="bank%d" % number, name=name)

        w_bf = keep.tile([P, 3], BF16, name="w_bf")
        nc.scalar.dma_start(out=w_bf[:], in_=w_p.rearrange("a b -> (a b)").partition_broadcast(P))
        x_sb = []
        for g in range(PASSES):
            x_rows = keep.tile([P, PACK, FEATS], BF16, name="x_sb%d" % g)
            nc.sync.dma_start(
                out=x_rows[:].rearrange("p (u e) d -> p u (e d)", e=2),
                in_=x_p[512 * g : 512 * (g + 1), :].rearrange("(u p e) d -> p u (e d)", u=2, e=2),
            )
            x_sb.append(x_rows)
        a_sb = []
        for c in range(PAIRS):
            a_rows = keep.tile([P, 2, NODES], BF16, name="a_sb%d" % c)
            nc.sync.dma_start(
                out=a_rows[:].rearrange("p e j -> p (e j)"),
                in_=A_p[256 * c : 256 * (c + 1), :].rearrange("(p e) j -> p (e j)", e=2),
            )
            a_sb.append(a_rows)
        ident = keep.tile([P, P], F32, name="ident")
        make_identity(nc, ident[:])
        w_f = keep.tile([P, 3], F32, name="w_f")
        nc.vector.tensor_copy(out=w_f[:], in_=w_bf[:])

        x_grouped = []
        x_codes = []
        x_scales = []

        def regroup_x(g):
            grouped = keep.tile([P, FEATS, PACK], BF16, name="x_grouped%d" % g, align_bytes=64)
            split = FEATS - X_SCALAR_COLS
            for copy, lo, hi in ((nc.vector.tensor_copy, 0, split), (nc.scalar.copy, split, FEATS)):
                copy(
                    out=grouped[:, lo:hi, :].rearrange("p (c i) t -> p c t i", i=4),
                    in_=x_sb[g][:, :, lo:hi].rearrange("p t (c i) -> p c t i", i=4),
                )
            x_grouped.append(grouped)

        def quantise_x(g):
            codes = keep.tile([P, FEATS], U32, name="x_codes%d" % g, align_bytes=64)
            scales = keep.tile([P, FEATS], U8, name="x_scales%d" % g, align_bytes=64)
            nc.vector.quantize_mx(
                out=codes[:].bitcast(FP8X4), scales=scales[:], in_=x_grouped[g][:].rearrange("p d t -> p (d t)")
            )
            x_codes.append(codes)
            x_scales.append(scales)

        w0_x = {}

        def scale_x(g, half):
            w0_x[(g, half)] = keep.tile([P, PACK, HALF], F32, name="w0_x%d%d" % (g, half))
            nc.vector.tensor_scalar(
                out=w0_x[(g, half)][:],
                in0=x_sb[g][:, :, HALF * half : HALF * (half + 1)],
                scalar1=w_f[:, 0:1],
                scalar2=None,
                op0=ALU.mult,
            )

        a_t = {}
        a_grouped = {}
        a_codes = {}
        a_scales = {}

        def transpose_tile(m):
            a_t[m] = bank(m, [P, 4, P], "a_t%d" % m)
            words = a_sb[m // 2][:, m % 2, :].bitcast(F32)
            for plane in range(4):
                nc.tensor.transpose(a_t[m][:, plane, :], words[:, P * plane : P * (plane + 1)], ident[:])

        def copy_tile(m):
            if m % 2 == 0:
                a_grouped[m // 2] = keep.tile([P, 2, NODES], BF16, name="a_grouped%d" % (m // 2), align_bytes=64)
            nc.scalar.copy(
                out=a_grouped[m // 2][:, m % 2, :].bitcast(F32).rearrange("p (g i u) -> p g i u", g=PASSES, u=2),
                in_=a_t[m][:].rearrange("p (g u) i -> p g i u", u=2),
            )

        def quantise_pair(c):
            a_codes[c] = keep.tile([P, 2 * PASSES * P], U32, name="a_codes%d" % c, align_bytes=64)
            a_scales[c] = keep.tile([P, 2 * PASSES * P], U8, name="a_scales%d" % c, align_bytes=64)
            nc.vector.quantize_mx(
                out=a_codes[c][:].bitcast(FP8X4),
                scales=a_scales[c][:],
                in_=a_grouped[c][:].rearrange("p e k -> p (e k)"),
            )

        def multiply(group, m, moving_codes, moving_scales):
            for g in range(PASSES):
                lo = (PASSES * (m % 2) + g) * P
                nc.tensor.matmul_mx(
                    out=group,
                    lhsT=a_codes[m // 2][:, lo : lo + P].bitcast(FP8X4),
                    lhsT_scale=a_scales[m // 2][:, lo : lo + P],
                    rhs=moving_codes[g].bitcast(FP8X4),
                    rhs_scale=moving_scales[g],
                    start=(g == 0),
                    stop=(g == PASSES - 1),
                )

        h1 = {}

        def first_product(m, half):
            g, t = divmod(m, PACK)
            for r in range(2):
                if t == 0:
                    h1[(g, half, r)] = bank(4 * half + 2 * g + r, [P, PACK, CHUNK], "h1_%d%d%d" % (g, half, r))
                cols = slice(HALF * half + CHUNK * r, HALF * half + CHUNK * (r + 1))
                multiply(h1[(g, half, r)][:, t, :], m, [c[:, cols] for c in x_codes], [s[:, cols] for s in x_scales])

        partial = {}
        h_codes = {}
        h_scales = {}

        def empty_h1(g, half):
            grouped = keep.tile([P, HALF, PACK], BF16, name="h_grouped%d%d" % (g, half), align_bytes=64)
            partial[(g, half)] = keep.tile([P, PACK, HALF], F32, name="partial%d%d" % (g, half))
            h_codes[(g, half)] = keep.tile([P, HALF], U32, name="h_codes%d%d" % (g, half), align_bytes=64)
            h_scales[(g, half)] = keep.tile([P, HALF], U8, name="h_scales%d%d" % (g, half), align_bytes=64)
            chunks = [slice(CHUNK * r, CHUNK * (r + 1)) for r in range(2)]

            def quantise_h1():
                nc.vector.quantize_mx(
                    out=h_codes[(g, half)][:].bitcast(FP8X4),
                    scales=h_scales[(g, half)][:],
                    in_=grouped[:].rearrange("p d t -> p (d t)"),
                )

            def add_on_vector(r):
                nc.vector.scalar_tensor_tensor(
                    out=partial[(g, half)][:, :, chunks[r]],
                    in0=h1[(g, half, r)][:],
                    scalar=w_f[:, 1:2],
                    in1=w0_x[(g, half)][:, :, chunks[r]],
                    op0=ALU.mult,
                    op1=ALU.add,
                )

            for r in range(2):
                nc.scalar.copy(out=grouped[:, chunks[r], :], in_=h1[(g, half, r)][:].rearrange("p t d -> p d t"))
            vector_chunks = [r for r in range(2) if r not in GPSIMD_CHUNKS[(g, half)]]
            for r in vector_chunks[:1]:
                add_on_vector(r)
            quantise_h1()
            for r in vector_chunks[1:]:
                add_on_vector(r)
            if GPSIMD_CHUNKS[(g, half)]:
                w1_h1 = keep.tile([P, 2, PACK, CHUNK], F32, name="w1_h1_%d%d" % (g, half))
            for r in GPSIMD_CHUNKS[(g, half)]:
                nc.scalar.activation(out=w1_h1[:, r], in_=h1[(g, half, r)][:], func=ACT.Copy, scale=w_f[:, 1:2])
            for r in GPSIMD_CHUNKS[(g, half)]:
                nc.gpsimd.tensor_tensor(
                    out=partial[(g, half)][:, :, chunks[r]],
                    in0=w1_h1[:, r],
                    in1=w0_x[(g, half)][:, :, chunks[r]],
                    op=ALU.add,
                )

        def second_product(half, c):
            h2 = bank(4 * half + c, [P, 2, HALF], "h2_%d%d" % (half, c))
            for e in range(2):
                multiply(
                    h2[:, e, :],
                    2 * c + e,
                    [h_codes[(g, half)][:] for g in range(PASSES)],
                    [h_scales[(g, half)][:] for g in range(PASSES)],
                )
            result = keep.tile([P, 2, HALF], F32, name="result%d%d" % (half, c))
            nc.vector.scalar_tensor_tensor(
                out=result[:],
                in0=h2[:],
                scalar=w_f[:, 2:3],
                in1=partial[(c // 2, half)][:, 2 * (c % 2) : 2 * (c % 2) + 2, :],
                op0=ALU.mult,
                op1=ALU.add,
            )
            nc.sync.dma_start(
                out=out[256 * c : 256 * (c + 1), HALF * half : HALF * (half + 1)].rearrange("(p e) d -> p e d", e=2),
                in_=result[:],
            )

        regroup_x(0)
        for half in range(2):
            scale_x(0, half)
        regroup_x(1)
        for g in range(PASSES):
            quantise_x(g)
        for c in range(PAIRS):
            for m in (2 * c, 2 * c + 1):
                transpose_tile(m)
            for m in (2 * c, 2 * c + 1):
                copy_tile(m)
            quantise_pair(c)
            if c < 2:
                scale_x(1, c)
        last_pair = (2 * PAIRS - 2, 2 * PAIRS - 1)
        for m in range(last_pair[0]):
            first_product(m, 0)
        for m in range(2):
            first_product(m, 1)
        for m in last_pair:
            first_product(m, 0)
        for g in range(PASSES):
            empty_h1(g, 0)
        for m in range(2, 2 * PAIRS):
            first_product(m, 1)
        for g in range(PASSES):
            empty_h1(g, 1)
        for half in range(2):
            for c in range(PAIRS):
                second_product(half, c)
